import numpy as np
import ml_dtypes


def mxq(x, axis, fmt="e4m3"):
    dtype, down = {"e4m3": (ml_dtypes.float8_e4m3fn, 7), "e5m2": (ml_dtypes.float8_e5m2, 14)}[fmt]
    v = np.moveaxis(np.asarray(x, np.float32).astype(ml_dtypes.bfloat16).astype(np.float64), axis, -1)
    blocks = v.reshape(v.shape[:-1] + (-1, 32))
    amax = np.abs(blocks).max(-1, keepdims=True)
    byte = np.maximum(np.where(amax > 0, np.frexp(amax)[1] - 1 + 127, 0) - down, 1)
    scale = np.exp2(byte - 127.0)
    codes = (blocks / scale).astype(np.float32).astype(dtype).astype(np.float64)
    return np.moveaxis((codes * scale).reshape(v.shape), -1, axis)


WIDE = False


def mx_kscale(k):
    if not WIDE:
        return np.ones(k)
    levels = np.array([10, -10, 5, -5, 0])
    if k % 512:
        return np.exp2(np.random.permutation(np.resize(levels, k // 32))).repeat(32)
    a = np.empty((k // 512, 16))
    for p in range(k // 512):
        a[p, :8] = np.random.permutation(np.resize(levels, 8))
        for g in range(8):
            far = levels[np.abs(levels - a[p, g]) >= 10]
            a[p, g + 8] = far[np.random.randint(len(far))]
    return np.exp2(a.ravel()).repeat(32)


BF16 = ml_dtypes.bfloat16


def bf(x):
    return np.asarray(x, np.float32).astype(BF16)


def f64(x):
    return np.asarray(x).astype(np.float64)


N, NFEAT, NHID, NOUT, NCLS = 1024, 512, 512, 512, 128
SPAN = 60.0
LAM = SPAN * np.log(2.0)
AGG = np.sqrt(LAM / (2.0 * N))


def setup_inputs():
    s, r = mx_kscale(NFEAT), mx_kscale(N)
    return {
        "x": bf(np.random.standard_normal((N, NFEAT)) * s / r[:, None]),
        "adj": bf(np.exp2(-SPAN * np.random.uniform(size=(N, N))) * (LAM / N) * r),
        "W1": bf(np.random.standard_normal((NFEAT, NHID)) * (0.7 / (AGG * np.sqrt(NFEAT))) / s[:, None]),
        "b1": bf(np.random.standard_normal(NHID) * 0.3),
    }


def reference(x, adj, W1, b1):
    support = mxq(f64(x), 1, "e4m3") @ mxq(f64(W1), 0, "e4m3")
    return np.maximum((mxq(f64(adj), 1, "e4m3") @ mxq(support, 0, "e4m3")) + f64(b1), 0.0)

@@ -1,0 +1,216 @@
+from contextlib import ExitStack
+
+import concourse.mybir as mybir
+from concourse.masks import make_identity
+
+NODES, FEAT, HID = 1024, 512, 512
+FLOPS = 2 * NODES * FEAT * HID + 2 * NODES * NODES * HID
+
+F32 = mybir.dt.float32
+BF16 = mybir.dt.bfloat16
+U32 = mybir.dt.uint32
+U8 = mybir.dt.uint8
+FP8X4 = mybir.dt.float8_e4m3fn_x4
+ADD = mybir.AluOpType.add
+MAX = mybir.AluOpType.max
+RELU = mybir.ActivationFunctionType.Relu
+
+P = 128
+PACK = 4
+BANK = 512
+SUPPORT_BANK_DT = F32
+
+
+def tile_gcn_pa_kernel(tc, x, adj, W1, b1, out):
+    nc = tc.nc
+    with ExitStack() as ctx:
+        keep = ctx.enter_context(tc.tile_pool(name="keep", bufs=1))
+        psum = ctx.enter_context(tc.psum_pool(name="psum", bufs=8))
+
+        def copy_on(engine, dst, src):
+            if engine == "S":
+                nc.scalar.copy(out=dst, in_=src)
+            else:
+                nc.vector.tensor_copy(out=dst, in_=src)
+
+        codes = {}
+        scales = {}
+
+        def quantize(name, grouped):
+            codes[name] = keep.tile([P, 512], U32, name=name + "_codes", align_bytes=64)
+            scales[name] = keep.tile([P, 512], U8, name=name + "_scales", align_bytes=64)
+            nc.vector.quantize_mx(out=codes[name][:].bitcast(FP8X4), scales=scales[name][:], in_=grouped)
+
+        def mx(acc, lhs, c0, rhs, start, stop):
+            nc.tensor.matmul_mx(
+                out=acc[:],
+                lhsT=codes[lhs][:, c0 : c0 + P].bitcast(FP8X4),
+                lhsT_scale=scales[lhs][:, c0 : c0 + P],
+                rhs=codes[rhs][:].bitcast(FP8X4),
+                rhs_scale=scales[rhs][:],
+                start=start,
+                stop=stop,
+            )
+
+        ident = keep.tile([P, P], F32, name="ident")
+        make_identity(nc, ident[:])
+        warm = keep.tile([P, 1], F32, name="warm")
+        nc.vector.memset(warm[:], 0.0)
+        nc.scalar.activation(out=warm[:], in_=warm[:], func=RELU)
+
+        w_raw = keep.tile([P, PACK, HID], BF16, name="w_raw")
+        w_grp = keep.tile([P, HID, PACK], BF16, name="w_grp", align_bytes=64)
+        x_sb = [[keep.tile([P, 2, FEAT], BF16, name="x_sb%d%d" % (g, b)) for b in range(2)] for g in range(2)]
+        x_grp = [keep.tile([P, PACK * 512], BF16, name="x_grp%d" % g, align_bytes=64) for g in range(2)]
+        adj_sb = [keep.tile([P, 2, NODES], BF16, name="adj_sb%d" % q) for q in range(4)]
+        adj_grp = [keep.tile([P, PACK * 512], BF16, name="adj_grp%d" % q, align_bytes=64) for q in range(4)]
+        sup_raw = [keep.tile([P, PACK, HID], BF16, name="sup_raw%d" % g) for g in range(2)]
+        sup_grp = [keep.tile([P, HID, PACK], BF16, name="sup_grp%d" % g, align_bytes=64) for g in range(2)]
+        bias = keep.tile([P, HID], BF16, name="bias")
+        o_sb = [keep.tile([P, 2, HID], F32, name="o_sb%d" % q) for q in range(4)]
+        adj_rows = adj.rearrange("(p r) k -> p r k", r=8)
+        out_rows = out.rearrange("(p r) h -> p r h", r=8)
+        banks = {}
+
+        def LW():
+            nc.sync.dma_start(out=w_raw[:], in_=W1.rearrange("(p j) c -> p j c", j=PACK))
+
+        def LX(g, b):
+            rows = x[512 * g : 512 * (g + 1), :].rearrange("(m t) k -> m t k", t=PACK)
+            nc.sync.dma_start(out=x_sb[g][b][:], in_=rows[:, 2 * b : 2 * b + 2, :])
+
+        def LA(q):
+            nc.sync.dma_start(out=adj_sb[q][:], in_=adj_rows[:, 2 * q : 2 * q + 2, :])
+
+        def LB():
+            nc.sync.dma_start(out=bias[:], in_=b1.partition_broadcast(P))
+
+        def WI(engine):
+            copy_on(engine, w_grp[:], w_raw[:].rearrange("p j c -> p c j"))
+
+        def QW():
+            quantize("w", w_grp[:].rearrange("p c j -> p (c j)"))
+
+        def XT(g, b):
+            xt = psum.tile([P, BANK], F32, name="xt", tag="bank")
+            banks["x%d%d" % (g, b)] = xt
+            for s in range(2):
+                words = x_sb[g][b][:, s, :].bitcast(F32)
+                for u in range(2):
+                    c0 = (2 * s + u) * P
+                    nc.tensor.transpose(xt[:, c0 : c0 + P], words[:, u : FEAT // 2 : 2], ident[:])
+
+        def XC(g, b, engine):
+            copy_on(
+                engine,
+                x_grp[g][:, 1024 * b : 1024 * (b + 1)].bitcast(F32).rearrange("p (s m u) -> p s m u", s=2, u=2),
+                banks["x%d%d" % (g, b)][:].rearrange("p (s u m) -> p s m u", s=2, u=2),
+            )
+
+        def QX(g):
+            quantize("x%d" % g, x_grp[g][:])
+
+        def AT(r):
+            at = psum.tile([P, BANK], F32, name="at", tag="bank")
+            banks["a%d" % r] = at
+            words = adj_sb[r // 2][:, r % 2, :].bitcast(F32)
+            for g in range(2):
+                for u in range(2):
+                    c0 = (2 * g + u) * P
+                    nc.tensor.transpose(at[:, c0 : c0 + P], words[:, 256 * g + u : 256 * (g + 1) : 2], ident[:])
+
+        def AC(r, engine):
+            e = r % 2
+            copy_on(
+                engine,
+                adj_grp[r // 2][:, 1024 * e : 1024 * (e + 1)].bitcast(F32).rearrange("p (g i u) -> p g i u", g=2, u=2),
+                banks["a%d" % r][:].rearrange("p (g u i) -> p g i u", g=2, u=2),
+            )
+
+        def QA(q):
+            quantize("a%d" % q, adj_grp[q][:])
+
+        def S1(g, t):
+            bank = psum.tile([P, BANK], SUPPORT_BANK_DT, name="sup_bank", tag="bank")
+            banks["s%d%d" % (g, t)] = bank
+            mx(bank, "x%d" % g, P * t, "w", True, True)
+
+        def SC(g, t, engine):
+            copy_on(engine, sup_raw[g][:, t, :], banks["s%d%d" % (g, t)][:])
+
+        def SI(g, engine):
+            copy_on(engine, sup_grp[g][:], sup_raw[g][:].rearrange("p t c -> p c t"))
+
+        def QS(g):
+            quantize("s%d" % g, sup_grp[g][:].rearrange("p c t -> p (c t)"))
+
+        def PP(r, g):
+            if g == 0:
+                banks["o%d" % r] = psum.tile([P, BANK], F32, name="acc", tag="bank")
+            mx(banks["o%d" % r], "a%d" % (r // 2), (2 * (r % 2) + g) * P, "s%d" % g, g == 0, g == 1)
+
+        def AD(r):
+            nc.vector.tensor_tensor(out=o_sb[r // 2][:, r % 2, :], in0=banks["o%d" % r][:], in1=bias[:], op=ADD)
+
+        def RL(r, engine):
+            o = o_sb[r // 2][:, r % 2, :]
+            if engine == "S":
+                nc.scalar.activation(out=o, in_=o, func=RELU)
+            else:
+                nc.gpsimd.tensor_scalar(out=o, in0=o, scalar1=0.0, scalar2=0.0, op0=MAX, op1=ADD)
+
+        def ST(r):
+            nc.sync.dma_start(out=out_rows[:, r, :], in_=o_sb[r // 2][:, r % 2, :])
+
+        ctx.enter_context(tc.manual_schedule())
+        LW()
+        LX(0, 0)
+        LX(0, 1)
+        LX(1, 0)
+        LX(1, 1)
+        for q in range(4):
+            LA(q)
+        LB()
+        WI("V")
+        QW()
+        XT(0, 0)
+        XC(0, 0, "S")
+        XT(0, 1)
+        XC(0, 1, "S")
+        QX(0)
+        XT(1, 0)
+        XC(1, 0, "S")
+        XT(1, 1)
+        XC(1, 1, "S")
+        QX(1)
+        for t in range(4):
+            S1(0, t)
+            SC(0, t, "SV"[t % 2])
+        for t in range(4):
+            S1(1, t)
+        for t in range(4):
+            SC(1, t, "S")
+        SI(0, "V")
+        QS(0)
+        for r in range(2):
+            AT(r)
+            AC(r, "S")
+        SI(1, "V")
+        QA(0)
+        QS(1)
+        for q in range(1, 4):
+            for r in (2 * q, 2 * q + 1):
+                AT(r)
+                AC(r, "S")
+            if q < 3:
+                QA(q)
+        for q in range(4):
+            for g in range(2):
+                PP(2 * q, g)
+                PP(2 * q + 1, g)
+            for r in (2 * q, 2 * q + 1):
+                AD(r)
+                RL(r, "S")
+                ST(r)
+            if q == 0:
+                QA(3)

@@ -162,6 +162,16 @@ def tile_gcn_pa_kernel(tc, x, adj, W1, b1, out):
         def ST(r):
             nc.sync.dma_start(out=out_rows[:, r, :], in_=o_sb[r // 2][:, r % 2, :])
 
+        def HEAT32(n):
+            heat = psum.tile([P, BANK], F32, name="heat", tag="bank")
+            for i in range(n):
+                nc.tensor.matmul(out=heat[:, 0:P], lhsT=ident[:], rhs=ident[:], start=True, stop=True)
+
+        def HEAT16(n):
+            heat = psum.tile([P, BANK], F32, name="heat", tag="bank")
+            for i in range(n):
+                nc.tensor.matmul(out=heat[:], lhsT=w_raw[:, 0, 0:P], rhs=w_raw[:, 0, :], start=True, stop=True)
+
         ctx.enter_context(tc.manual_schedule())
         LW()
         LX(0, 0)
@@ -171,6 +181,8 @@ def tile_gcn_pa_kernel(tc, x, adj, W1, b1, out):
         for q in range(4):
             LA(q)
         LB()
+        HEAT32(4)
+        HEAT16(2)
         WI("V")
         QW()
         XT(0, 0)
@@ -178,11 +190,13 @@ def tile_gcn_pa_kernel(tc, x, adj, W1, b1, out):
         XT(0, 1)
         XC(0, 1, "S")
         QX(0)
+        HEAT16(1)
         XT(1, 0)
         XC(1, 0, "S")
         XT(1, 1)
         XC(1, 1, "S")
         QX(1)
+        HEAT16(1)
         for t in range(4):
             S1(0, t)
             SC(0, t, "SV"[t % 2])
@@ -195,22 +209,26 @@ def tile_gcn_pa_kernel(tc, x, adj, W1, b1, out):
         for r in range(2):
             AT(r)
             AC(r, "S")
+        HEAT16(2)
         SI(1, "V")
         QA(0)
         QS(1)
-        for q in range(1, 4):
-            for r in (2 * q, 2 * q + 1):
-                AT(r)
-                AC(r, "S")
-            if q < 3:
-                QA(q)
-        for q in range(4):
-            for g in range(2):
-                PP(2 * q, g)
-                PP(2 * q + 1, g)
-            for r in (2 * q, 2 * q + 1):
-                AD(r)
-                RL(r, "S")
-                ST(r)
-            if q == 0:
+        for r in range(2, 5):
+            AT(r)
+            AC(r, "S")
+            if r == 3:
+                QA(1)
+        HEAT16(2)
+        for r in range(5, 8):
+            AT(r)
+            AC(r, "S")
+            if r == 5:
+                QA(2)
+        for r in range(8):
+            PP(r, 0)
+            PP(r, 1)
+            AD(r)
+            RL(r, "S")
+            ST(r)
+            if r == 1:
                 QA(3)

from contextlib import ExitStack

import concourse.mybir as mybir
from concourse.masks import make_identity

NODES, FEAT, HID = 1024, 512, 512
FLOPS = 2 * NODES * FEAT * HID + 2 * NODES * NODES * HID

F32 = mybir.dt.float32
BF16 = mybir.dt.bfloat16
U32 = mybir.dt.uint32
U8 = mybir.dt.uint8
FP8X4 = mybir.dt.float8_e4m3fn_x4
ADD = mybir.AluOpType.add
MAX = mybir.AluOpType.max
RELU = mybir.ActivationFunctionType.Relu

P = 128
PACK = 4
BANK = 512
SUPPORT_BANK_DT = F32


def tile_gcn_pa_kernel(tc, x, adj, W1, b1, out):
    nc = tc.nc
    with ExitStack() as ctx:
        keep = ctx.enter_context(tc.tile_pool(name="keep", bufs=1))
        psum = ctx.enter_context(tc.psum_pool(name="psum", bufs=8))

        def copy_on(engine, dst, src):
            if engine == "S":
                nc.scalar.copy(out=dst, in_=src)
            else:
                nc.vector.tensor_copy(out=dst, in_=src)

        codes = {}
        scales = {}

        def quantize(name, grouped):
            codes[name] = keep.tile([P, 512], U32, name=name + "_codes", align_bytes=64)
            scales[name] = keep.tile([P, 512], U8, name=name + "_scales", align_bytes=64)
            nc.vector.quantize_mx(out=codes[name][:].bitcast(FP8X4), scales=scales[name][:], in_=grouped)

        def mx(acc, lhs, c0, rhs, start, stop):
            nc.tensor.matmul_mx(
                out=acc[:],
                lhsT=codes[lhs][:, c0 : c0 + P].bitcast(FP8X4),
                lhsT_scale=scales[lhs][:, c0 : c0 + P],
                rhs=codes[rhs][:].bitcast(FP8X4),
                rhs_scale=scales[rhs][:],
                start=start,
                stop=stop,
            )

        ident = keep.tile([P, P], F32, name="ident")
        make_identity(nc, ident[:])
        warm = keep.tile([P, 1], F32, name="warm")
        nc.vector.memset(warm[:], 0.0)
        nc.scalar.activation(out=warm[:], in_=warm[:], func=RELU)

        w_raw = keep.tile([P, PACK, HID], BF16, name="w_raw")
        w_grp = keep.tile([P, HID, PACK], BF16, name="w_grp", align_bytes=64)
        x_sb = [[keep.tile([P, 2, FEAT], BF16, name="x_sb%d%d" % (g, b)) for b in range(2)] for g in range(2)]
        x_grp = [keep.tile([P, PACK * 512], BF16, name="x_grp%d" % g, align_bytes=64) for g in range(2)]
        adj_sb = [keep.tile([P, 2, NODES], BF16, name="adj_sb%d" % q) for q in range(4)]
        adj_grp = [keep.tile([P, PACK * 512], BF16, name="adj_grp%d" % q, align_bytes=64) for q in range(4)]
        sup_raw = [keep.tile([P, PACK, HID], BF16, name="sup_raw%d" % g) for g in range(2)]
        sup_grp = [keep.tile([P, HID, PACK], BF16, name="sup_grp%d" % g, align_bytes=64) for g in range(2)]
        bias = keep.tile([P, HID], BF16, name="bias")
        o_sb = [keep.tile([P, 2, HID], F32, name="o_sb%d" % q) for q in range(4)]
        adj_rows = adj.rearrange("(p r) k -> p r k", r=8)
        out_rows = out.rearrange("(p r) h -> p r h", r=8)
        banks = {}

        def LW():
            nc.sync.dma_start(out=w_raw[:], in_=W1.rearrange("(p j) c -> p j c", j=PACK))

        def LX(g, b):
            rows = x[512 * g : 512 * (g + 1), :].rearrange("(m t) k -> m t k", t=PACK)
            nc.sync.dma_start(out=x_sb[g][b][:], in_=rows[:, 2 * b : 2 * b + 2, :])

        def LA(q):
            nc.sync.dma_start(out=adj_sb[q][:], in_=adj_rows[:, 2 * q : 2 * q + 2, :])

        def LB():
            nc.sync.dma_start(out=bias[:], in_=b1.partition_broadcast(P))

        def WI(engine):
            copy_on(engine, w_grp[:], w_raw[:].rearrange("p j c -> p c j"))

        def QW():
            quantize("w", w_grp[:].rearrange("p c j -> p (c j)"))

        def XT(g, b):
            xt = psum.tile([P, BANK], F32, name="xt", tag="bank")
            banks["x%d%d" % (g, b)] = xt
            for s in range(2):
                words = x_sb[g][b][:, s, :].bitcast(F32)
                for u in range(2):
                    c0 = (2 * s + u) * P
                    nc.tensor.transpose(xt[:, c0 : c0 + P], words[:, u : FEAT // 2 : 2], ident[:])

        def XC(g, b, engine):
            copy_on(
                engine,
                x_grp[g][:, 1024 * b : 1024 * (b + 1)].bitcast(F32).rearrange("p (s m u) -> p s m u", s=2, u=2),
                banks["x%d%d" % (g, b)][:].rearrange("p (s u m) -> p s m u", s=2, u=2),
            )

        def QX(g):
            quantize("x%d" % g, x_grp[g][:])

        def AT(r):
            at = psum.tile([P, BANK], F32, name="at", tag="bank")
            banks["a%d" % r] = at
            words = adj_sb[r // 2][:, r % 2, :].bitcast(F32)
            for g in range(2):
                for u in range(2):
                    c0 = (2 * g + u) * P
                    nc.tensor.transpose(at[:, c0 : c0 + P], words[:, 256 * g + u : 256 * (g + 1) : 2], ident[:])

        def AC(r, engine):
            e = r % 2
            copy_on(
                engine,
                adj_grp[r // 2][:, 1024 * e : 1024 * (e + 1)].bitcast(F32).rearrange("p (g i u) -> p g i u", g=2, u=2),
                banks["a%d" % r][:].rearrange("p (g u i) -> p g i u", g=2, u=2),
            )

        def QA(q):
            quantize("a%d" % q, adj_grp[q][:])

        def S1(g, t):
            bank = psum.tile([P, BANK], SUPPORT_BANK_DT, name="sup_bank", tag="bank")
            banks["s%d%d" % (g, t)] = bank
            mx(bank, "x%d" % g, P * t, "w", True, True)

        def SC(g, t, engine):
            copy_on(engine, sup_raw[g][:, t, :], banks["s%d%d" % (g, t)][:])

        def SI(g, engine):
            copy_on(engine, sup_grp[g][:], sup_raw[g][:].rearrange("p t c -> p c t"))

        def QS(g):
            quantize("s%d" % g, sup_grp[g][:].rearrange("p c t -> p (c t)"))

        def PP(r, g):
            if g == 0:
                banks["o%d" % r] = psum.tile([P, BANK], F32, name="acc", tag="bank")
            mx(banks["o%d" % r], "a%d" % (r // 2), (2 * (r % 2) + g) * P, "s%d" % g, g == 0, g == 1)

        def AD(r):
            nc.vector.tensor_tensor(out=o_sb[r // 2][:, r % 2, :], in0=banks["o%d" % r][:], in1=bias[:], op=ADD)

        def RL(r, engine):
            o = o_sb[r // 2][:, r % 2, :]
            if engine == "S":
                nc.scalar.activation(out=o, in_=o, func=RELU)
            else:
                nc.gpsimd.tensor_scalar(out=o, in0=o, scalar1=0.0, scalar2=0.0, op0=MAX, op1=ADD)

        def ST(r):
            nc.sync.dma_start(out=out_rows[:, r, :], in_=o_sb[r // 2][:, r % 2, :])

        def HEAT32(n):
            heat = psum.tile([P, BANK], F32, name="heat", tag="bank")
            for i in range(n):
                nc.tensor.matmul(out=heat[:, 0:P], lhsT=ident[:], rhs=ident[:], start=True, stop=True)

        def HEAT16(n):
            heat = psum.tile([P, BANK], F32, name="heat", tag="bank")
            for i in range(n):
                nc.tensor.matmul(out=heat[:], lhsT=w_raw[:, 0, 0:P], rhs=w_raw[:, 0, :], start=True, stop=True)

        ctx.enter_context(tc.manual_schedule())
        LW()
        LX(0, 0)
        LX(0, 1)
        LX(1, 0)
        LX(1, 1)
        for q in range(4):
            LA(q)
        LB()
        HEAT32(4)
        HEAT16(2)
        WI("V")
        QW()
        XT(0, 0)
        XC(0, 0, "S")
        XT(0, 1)
        XC(0, 1, "S")
        QX(0)
        HEAT16(1)
        XT(1, 0)
        XC(1, 0, "S")
        XT(1, 1)
        XC(1, 1, "S")
        QX(1)
        HEAT16(1)
        for t in range(4):
            S1(0, t)
            SC(0, t, "SV"[t % 2])
        for t in range(4):
            S1(1, t)
        for t in range(4):
            SC(1, t, "S")
        SI(0, "V")
        QS(0)
        for r in range(2):
            AT(r)
            AC(r, "S")
        HEAT16(2)
        SI(1, "V")
        QA(0)
        QS(1)
        for r in range(2, 5):
            AT(r)
            AC(r, "S")
            if r == 3:
                QA(1)
        HEAT16(2)
        for r in range(5, 8):
            AT(r)
            AC(r, "S")
            if r == 5:
                QA(2)
        for r in range(8):
            PP(r, 0)
            PP(r, 1)
            AD(r)
            RL(r, "S")
            ST(r)
            if r == 1:
                QA(3)
